import numpy as np
import ml_dtypes


def mxq(x, axis, fmt="e4m3"):
    dtype, down = {"e4m3": (ml_dtypes.float8_e4m3fn, 7), "e5m2": (ml_dtypes.float8_e5m2, 14)}[fmt]
    v = np.moveaxis(np.asarray(x, np.float32).astype(ml_dtypes.bfloat16).astype(np.float64), axis, -1)
    blocks = v.reshape(v.shape[:-1] + (-1, 32))
    amax = np.abs(blocks).max(-1, keepdims=True)
    byte = np.maximum(np.where(amax > 0, np.frexp(amax)[1] - 1 + 127, 0) - down, 1)
    scale = np.exp2(byte - 127.0)
    codes = (blocks / scale).astype(np.float32).astype(dtype).astype(np.float64)
    return np.moveaxis((codes * scale).reshape(v.shape), -1, axis)


WIDE = False


def mx_kscale(k):
    if not WIDE:
        return np.ones(k)
    levels = np.array([10, -10, 5, -5, 0])
    a = np.random.permutation(np.resize(levels, k // 512 * 4)).reshape(k // 512, 4)
    idx = np.arange(k)
    return np.exp2(a[idx // 512, idx % 128 // 32])


BF16 = ml_dtypes.bfloat16


def bf(x):
    return np.asarray(x, np.float32).astype(BF16)


def f64(x):
    return np.asarray(x).astype(np.float64)


B, N, D, F, C, L = 1024, 4096, 1024, 1024, 128, 28
EPS = 1e-12


def l2norm(x):
    n = np.sqrt(np.sum(x * x, axis=1, keepdims=True))
    return x / np.maximum(n, EPS)


def setup_inputs():
    s = mx_kscale(D)
    return {"features": bf(np.random.standard_normal((B, D)) * s),
            "ex_features": bf(np.random.standard_normal((N, D)) * s),
            "g_weight": bf(np.random.standard_normal((F, D)) / np.sqrt(D) / s)}


def reference(features, ex_features, g_weight):
    gq = mxq(f64(g_weight), 1, "e4m3")
    f = mxq(f64(features), 1, "e4m3") @ gq.T
    exf = mxq(f64(ex_features), 1, "e4m3") @ gq.T
    return l2norm(f), l2norm(exf)

@@ -1,0 +1,206 @@
+from contextlib import ExitStack
+
+import concourse.mybir as mybir
+from concourse.masks import make_identity
+
+F32 = mybir.dt.float32
+BF16 = mybir.dt.bfloat16
+U32 = mybir.dt.uint32
+U8 = mybir.dt.uint8
+FP8X4 = mybir.dt.float8_e4m3fn_x4
+ACT = mybir.ActivationFunctionType
+ALU = mybir.AluOpType
+
+P = 128
+PACK = 4
+K = 1024
+K_PASS = P * PACK
+PASSES = K // K_PASS
+F_OUT = 1024
+N_TILE = 512
+HALVES = F_OUT // N_TILE
+W_TILES = F_OUT // P
+PAIR = 2
+PLANES = K // 2 // P
+TILE_WORDS = PASSES * P
+X_AHEAD = 6
+EPS = 1e-12
+
+FLOPS = 2 * (1024 + 4096) * K * F_OUT
+
+
+def tile_minerva_old_pa_kernel(tc, features, ex_features, g_weight, out_0, out_1):
+    nc = tc.nc
+
+    x_pairs = []
+    out_pairs = []
+    for x, out in ((features, out_0), (ex_features, out_1)):
+        x_view = x.rearrange("(q p a) k -> q p a k", p=P, a=PAIR)
+        out_view = out.rearrange("(q p a) f -> q p a f", p=P, a=PAIR)
+        for q in range(x.shape[0] // (P * PAIR)):
+            x_pairs.append(x_view[q])
+            out_pairs.append(out_view[q])
+    n_pairs = len(x_pairs)
+    n_tiles = n_pairs * PAIR
+    w_rows = g_weight.rearrange("(j p) k -> j p k", p=P)
+
+    with ExitStack() as ctx:
+        ctx.enter_context(tc.manual_schedule())
+        const = ctx.enter_context(tc.tile_pool(name="const", bufs=1))
+        w_in = ctx.enter_context(tc.tile_pool(name="w_in", bufs=W_TILES))
+        x_in = ctx.enter_context(tc.tile_pool(name="x_in", bufs=X_AHEAD))
+        stage = ctx.enter_context(tc.tile_pool(name="stage", bufs=3))
+        small = ctx.enter_context(tc.tile_pool(name="small", bufs=4))
+        result = ctx.enter_context(tc.tile_pool(name="result", bufs=6))
+        psum_t = ctx.enter_context(tc.psum_pool(name="psum_t", bufs=2))
+        psum_y = ctx.enter_context(tc.psum_pool(name="psum_y", bufs=6))
+
+        ident = const.tile([P, P], F32, name="ident")
+        make_identity(nc, ident[:])
+        neg_half = const.tile([P, 1], F32, name="neg_half")
+        nc.gpsimd.memset(neg_half[:], -0.5)
+
+        w_grouped = const.tile([P, PASSES * F_OUT * PACK], BF16, name="w_grouped", align_bytes=64)
+        w_codes = const.tile([P, PASSES * F_OUT], U32, name="w_codes", align_bytes=64)
+        w_scales = const.tile([P, PASSES * F_OUT], U8, name="w_scales", align_bytes=64)
+
+        w_raw = {}
+        x_raw = {}
+        banks = {}
+        grouped = {}
+        codes = {}
+        scales = {}
+        y = {}
+        sumsq = {}
+        rnorm = {}
+
+        def load_w(j):
+            w_raw[j] = w_in.tile([P, K], BF16, name="w_raw")
+            nc.sync.dma_start(out=w_raw[j][:], in_=w_rows[j])
+
+        def load_pair(q):
+            x_raw[q] = x_in.tile([P, PAIR, K], BF16, name="x_raw")
+            nc.sync.dma_start(out=x_raw[q][:], in_=x_pairs[q])
+
+        def transpose_words(rows):
+            bank = psum_t.tile([P, PLANES, P], F32, name="bank")
+            words = rows.bitcast(F32)
+            for c in range(PLANES):
+                nc.tensor.transpose(bank[:, c, :], words[:, c * P : (c + 1) * P], ident[:])
+            return bank
+
+        def by_row(bank):
+            return bank[:].rearrange("p (g u) r -> p g r u", u=2)
+
+        def prepare_weights(h):
+            dest = w_grouped[:].bitcast(F32).rearrange("p (g f u) -> p g f u", g=PASSES, u=2)
+            for j in range(h * W_TILES // HALVES, (h + 1) * W_TILES // HALVES):
+                bank = transpose_words(w_raw[j][:])
+                if j % 2 == 0:
+                    nc.vector.tensor_copy(out=dest[:, :, j * P : (j + 1) * P, :], in_=by_row(bank))
+                else:
+                    nc.scalar.copy(out=dest[:, :, j * P : (j + 1) * P, :], in_=by_row(bank))
+            for g in range(PASSES):
+                lo = g * F_OUT + h * N_TILE
+                nc.vector.quantize_mx(
+                    out=w_codes[:, lo : lo + N_TILE].bitcast(FP8X4),
+                    scales=w_scales[:, lo : lo + N_TILE],
+                    in_=w_grouped[:, lo * PACK : (lo + N_TILE) * PACK],
+                )
+
+        def transposes(q):
+            banks[q] = [transpose_words(x_raw[q][:, a, :]) for a in range(PAIR)]
+
+        def regroup(q):
+            grouped[q] = stage.tile([P, PAIR * TILE_WORDS * PACK], BF16, name="grouped", align_bytes=64)
+            dest = grouped[q][:].bitcast(F32).rearrange("p (a g r u) -> p a g r u", a=PAIR, g=PASSES, u=2)
+            for a in range(PAIR):
+                nc.vector.tensor_copy(out=dest[:, a], in_=by_row(banks[q][a]))
+
+        def quantise(q):
+            codes[q] = stage.tile([P, PAIR * TILE_WORDS], U32, name="codes", align_bytes=64)
+            scales[q] = stage.tile([P, PAIR * TILE_WORDS], U8, name="scales", align_bytes=64)
+            nc.vector.quantize_mx(
+                out=codes[q][:].bitcast(FP8X4), scales=scales[q][:], in_=grouped[q][:]
+            )
+
+        def multiply(i):
+            q, a = divmod(i, PAIR)
+            y[i] = []
+            for h in range(HALVES):
+                acc = psum_y.tile([P, N_TILE], F32, name="acc")
+                for g in range(PASSES):
+                    rows = slice(a * TILE_WORDS + g * P, a * TILE_WORDS + (g + 1) * P)
+                    cols = slice(g * F_OUT + h * N_TILE, g * F_OUT + (h + 1) * N_TILE)
+                    nc.tensor.matmul_mx(
+                        out=acc[:],
+                        lhsT=codes[q][:, rows].bitcast(FP8X4),
+                        lhsT_scale=scales[q][:, rows],
+                        rhs=w_codes[:, cols].bitcast(FP8X4),
+                        rhs_scale=w_scales[:, cols],
+                        start=(g == 0),
+                        stop=(g == PASSES - 1),
+                    )
+                y[i].append(acc)
+
+        def norm(i):
+            sumsq[i] = small.tile([P, HALVES], F32, name="sumsq")
+            for h in range(HALVES):
+                squares = stage.tile([P, N_TILE], F32, name="squares")
+                nc.scalar.activation(
+                    out=squares[:], in_=y[i][h][:], func=ACT.Square, accum_out=sumsq[i][:, h : h + 1]
+                )
+            clamped = small.tile([P, 1], F32, name="clamped")
+            nc.gpsimd.tensor_scalar(
+                out=clamped[:],
+                in0=sumsq[i][:, 0:1],
+                scalar1=sumsq[i][:, 1:2],
+                scalar2=EPS * EPS,
+                op0=ALU.add,
+                op1=ALU.max,
+            )
+            rnorm[i] = small.tile([P, 1], F32, name="rnorm")
+            nc.gpsimd.tensor_tensor(out=rnorm[i][:], in0=clamped[:], in1=neg_half[:], op=ALU.pow)
+
+        def scale_and_store(i):
+            q, a = divmod(i, PAIR)
+            unit = result.tile([P, F_OUT], F32, name="unit")
+            nc.vector.tensor_scalar(
+                out=unit[:, 0:N_TILE], in0=y[i][0][:], scalar1=rnorm[i][:, 0:1], scalar2=None, op0=ALU.mult
+            )
+            nc.scalar.activation(
+                out=unit[:, N_TILE:F_OUT], in_=y[i][1][:], func=ACT.Copy, scale=rnorm[i][:, 0:1]
+            )
+            nc.sync.dma_start(out=out_pairs[q][:, a, :], in_=unit[:])
+
+        for j in range(W_TILES // HALVES):
+            load_w(j)
+        load_pair(0)
+        for j in range(W_TILES // HALVES, W_TILES):
+            load_w(j)
+        for q in range(1, X_AHEAD):
+            load_pair(q)
+
+        prepare_weights(0)
+        transposes(0)
+        regroup(0)
+        prepare_weights(1)
+        transposes(1)
+        regroup(1)
+        quantise(0)
+
+        for i in range(n_tiles):
+            q, a = divmod(i, PAIR)
+            if a == 0:
+                if q + X_AHEAD < n_pairs:
+                    load_pair(q + X_AHEAD)
+                if q + 2 < n_pairs:
+                    transposes(q + 2)
+                    regroup(q + 2)
+                if q + 1 < n_pairs:
+                    quantise(q + 1)
+            multiply(i)
+            norm(i)
+            if i >= 1:
+                scale_and_store(i - 1)
+        scale_and_store(n_tiles - 1)

@@ -82,12 +82,10 @@ def tile_minerva_old_pa_kernel(tc, features, ex_features, g_weight, out_0, out_1
             x_raw[q] = x_in.tile([P, PAIR, K], BF16, name="x_raw")
             nc.sync.dma_start(out=x_raw[q][:], in_=x_pairs[q])
 
-        def transpose_words(rows):
-            bank = psum_t.tile([P, PLANES, P], F32, name="bank")
+        def transpose_words(rows, bank):
             words = rows.bitcast(F32)
             for c in range(PLANES):
                 nc.tensor.transpose(bank[:, c, :], words[:, c * P : (c + 1) * P], ident[:])
-            return bank
 
         def by_row(bank):
             return bank[:].rearrange("p (g u) r -> p g r u", u=2)
@@ -95,27 +93,32 @@ def tile_minerva_old_pa_kernel(tc, features, ex_features, g_weight, out_0, out_1
         def prepare_weights(h):
             dest = w_grouped[:].bitcast(F32).rearrange("p (g f u) -> p g f u", g=PASSES, u=2)
             for j in range(h * W_TILES // HALVES, (h + 1) * W_TILES // HALVES):
-                bank = transpose_words(w_raw[j][:])
-                if j % 2 == 0:
-                    nc.vector.tensor_copy(out=dest[:, :, j * P : (j + 1) * P, :], in_=by_row(bank))
-                else:
-                    nc.scalar.copy(out=dest[:, :, j * P : (j + 1) * P, :], in_=by_row(bank))
-            for g in range(PASSES):
-                lo = g * F_OUT + h * N_TILE
-                nc.vector.quantize_mx(
-                    out=w_codes[:, lo : lo + N_TILE].bitcast(FP8X4),
-                    scales=w_scales[:, lo : lo + N_TILE],
-                    in_=w_grouped[:, lo * PACK : (lo + N_TILE) * PACK],
-                )
+                bank = psum_y.tile([P, PLANES, P], F32, name="w_bank", tag="acc")
+                transpose_words(w_raw[j][:], bank)
+                nc.scalar.copy(out=dest[:, :, j * P : (j + 1) * P, :], in_=by_row(bank))
+                for g in range(PASSES):
+                    lo = g * F_OUT + j * P
+                    nc.vector.quantize_mx(
+                        out=w_codes[:, lo : lo + P].bitcast(FP8X4),
+                        scales=w_scales[:, lo : lo + P],
+                        in_=w_grouped[:, lo * PACK : (lo + P) * PACK],
+                    )
 
         def transposes(q):
-            banks[q] = [transpose_words(x_raw[q][:, a, :]) for a in range(PAIR)]
+            banks[q] = []
+            for a in range(PAIR):
+                bank = psum_t.tile([P, PLANES, P], F32, name="bank")
+                transpose_words(x_raw[q][:, a, :], bank)
+                banks[q].append(bank)
 
         def regroup(q):
             grouped[q] = stage.tile([P, PAIR * TILE_WORDS * PACK], BF16, name="grouped", align_bytes=64)
             dest = grouped[q][:].bitcast(F32).rearrange("p (a g r u) -> p a g r u", a=PAIR, g=PASSES, u=2)
             for a in range(PAIR):
-                nc.vector.tensor_copy(out=dest[:, a], in_=by_row(banks[q][a]))
+                if (q * PAIR + a) % 4 == 0:
+                    nc.vector.tensor_copy(out=dest[:, a], in_=by_row(banks[q][a]))
+                else:
+                    nc.scalar.copy(out=dest[:, a], in_=by_row(banks[q][a]))
 
         def quantise(q):
             codes[q] = stage.tile([P, PAIR * TILE_WORDS], U32, name="codes", align_bytes=64)
@@ -165,12 +168,14 @@ def tile_minerva_old_pa_kernel(tc, features, ex_features, g_weight, out_0, out_1
         def scale_and_store(i):
             q, a = divmod(i, PAIR)
             unit = result.tile([P, F_OUT], F32, name="unit")
-            nc.vector.tensor_scalar(
-                out=unit[:, 0:N_TILE], in0=y[i][0][:], scalar1=rnorm[i][:, 0:1], scalar2=None, op0=ALU.mult
-            )
-            nc.scalar.activation(
-                out=unit[:, N_TILE:F_OUT], in_=y[i][1][:], func=ACT.Copy, scale=rnorm[i][:, 0:1]
-            )
+            for h in range(HALVES):
+                nc.vector.tensor_scalar(
+                    out=unit[:, h * N_TILE : (h + 1) * N_TILE],
+                    in0=y[i][h][:],
+                    scalar1=rnorm[i][:, 0:1],
+                    scalar2=None,
+                    op0=ALU.mult,
+                )
             nc.sync.dma_start(out=out_pairs[q][:, a, :], in_=unit[:])
 
         for j in range(W_TILES // HALVES):
@@ -184,23 +189,24 @@ def tile_minerva_old_pa_kernel(tc, features, ex_features, g_weight, out_0, out_1
         prepare_weights(0)
         transposes(0)
         regroup(0)
+        quantise(0)
         prepare_weights(1)
         transposes(1)
         regroup(1)
-        quantise(0)
 
         for i in range(n_tiles):
             q, a = divmod(i, PAIR)
+            multiply(i)
+            norm(i)
             if a == 0:
                 if q + X_AHEAD < n_pairs:
                     load_pair(q + X_AHEAD)
                 if q + 2 < n_pairs:
                     transposes(q + 2)
-                    regroup(q + 2)
                 if q + 1 < n_pairs:
                     quantise(q + 1)
-            multiply(i)
-            norm(i)
             if i >= 1:
                 scale_and_store(i - 1)
+            if a == 0 and q + 2 < n_pairs:
+                regroup(q + 2)
         scale_and_store(n_tiles - 1)

@@ -21,9 +21,9 @@ N_TILE = 512
 HALVES = F_OUT // N_TILE
 W_TILES = F_OUT // P
 PAIR = 2
+BLOCK = 4
 PLANES = K // 2 // P
 TILE_WORDS = PASSES * P
-X_AHEAD = 6
 EPS = 1e-12
 
 FLOPS = 2 * (1024 + 4096) * K * F_OUT
@@ -32,23 +32,24 @@ FLOPS = 2 * (1024 + 4096) * K * F_OUT
 def tile_minerva_old_pa_kernel(tc, features, ex_features, g_weight, out_0, out_1):
     nc = tc.nc
 
-    x_pairs = []
-    out_pairs = []
+    x_blocks = []
+    out_blocks = []
     for x, out in ((features, out_0), (ex_features, out_1)):
-        x_view = x.rearrange("(q p a) k -> q p a k", p=P, a=PAIR)
-        out_view = out.rearrange("(q p a) f -> q p a f", p=P, a=PAIR)
-        for q in range(x.shape[0] // (P * PAIR)):
-            x_pairs.append(x_view[q])
-            out_pairs.append(out_view[q])
-    n_pairs = len(x_pairs)
-    n_tiles = n_pairs * PAIR
+        x_view = x.rearrange("(b p t) k -> b p t k", p=P, t=BLOCK)
+        out_view = out.rearrange("(b p t) f -> b p t f", p=P, t=BLOCK)
+        for b in range(x.shape[0] // (P * BLOCK)):
+            x_blocks.append(x_view[b])
+            out_blocks.append(out_view[b])
+    n_blocks = len(x_blocks)
+    n_tiles = n_blocks * BLOCK
+    n_pairs = n_tiles // PAIR
     w_rows = g_weight.rearrange("(j p) k -> j p k", p=P)
 
     with ExitStack() as ctx:
         ctx.enter_context(tc.manual_schedule())
         const = ctx.enter_context(tc.tile_pool(name="const", bufs=1))
         w_in = ctx.enter_context(tc.tile_pool(name="w_in", bufs=W_TILES))
-        x_in = ctx.enter_context(tc.tile_pool(name="x_in", bufs=X_AHEAD))
+        x_in = ctx.enter_context(tc.tile_pool(name="x_in", bufs=n_blocks))
         stage = ctx.enter_context(tc.tile_pool(name="stage", bufs=3))
         small = ctx.enter_context(tc.tile_pool(name="small", bufs=4))
         result = ctx.enter_context(tc.tile_pool(name="result", bufs=6))
@@ -73,14 +74,14 @@ def tile_minerva_old_pa_kernel(tc, features, ex_features, g_weight, out_0, out_1
         y = {}
         sumsq = {}
         rnorm = {}
+        unit = {}
 
         def load_w(j):
             w_raw[j] = w_in.tile([P, K], BF16, name="w_raw")
             nc.sync.dma_start(out=w_raw[j][:], in_=w_rows[j])
 
-        def load_pair(q):
-            x_raw[q] = x_in.tile([P, PAIR, K], BF16, name="x_raw")
-            nc.sync.dma_start(out=x_raw[q][:], in_=x_pairs[q])
+        def load_rows(b, t_lo, t_hi):
+            nc.sync.dma_start(out=x_raw[b][:, t_lo:t_hi, :], in_=x_blocks[b][:, t_lo:t_hi, :])
 
         def transpose_words(rows, bank):
             words = rows.bitcast(F32)
@@ -95,7 +96,10 @@ def tile_minerva_old_pa_kernel(tc, features, ex_features, g_weight, out_0, out_1
             for j in range(h * W_TILES // HALVES, (h + 1) * W_TILES // HALVES):
                 bank = psum_y.tile([P, PLANES, P], F32, name="w_bank", tag="acc")
                 transpose_words(w_raw[j][:], bank)
-                nc.scalar.copy(out=dest[:, :, j * P : (j + 1) * P, :], in_=by_row(bank))
+                if j % 2 == 0:
+                    nc.vector.tensor_copy(out=dest[:, :, j * P : (j + 1) * P, :], in_=by_row(bank))
+                else:
+                    nc.scalar.copy(out=dest[:, :, j * P : (j + 1) * P, :], in_=by_row(bank))
                 for g in range(PASSES):
                     lo = g * F_OUT + j * P
                     nc.vector.quantize_mx(
@@ -108,7 +112,8 @@ def tile_minerva_old_pa_kernel(tc, features, ex_features, g_weight, out_0, out_1
             banks[q] = []
             for a in range(PAIR):
                 bank = psum_t.tile([P, PLANES, P], F32, name="bank")
-                transpose_words(x_raw[q][:, a, :], bank)
+                b, t = divmod(q * PAIR + a, BLOCK)
+                transpose_words(x_raw[b][:, t, :], bank)
                 banks[q].append(bank)
 
         def regroup(q):
@@ -167,24 +172,32 @@ def tile_minerva_old_pa_kernel(tc, features, ex_features, g_weight, out_0, out_1
 
         def scale_and_store(i):
             q, a = divmod(i, PAIR)
-            unit = result.tile([P, F_OUT], F32, name="unit")
+            b, t = divmod(i, BLOCK)
+            if a == 0:
+                unit[q] = result.tile([P, PAIR, F_OUT], F32, name="unit")
             for h in range(HALVES):
                 nc.vector.tensor_scalar(
-                    out=unit[:, h * N_TILE : (h + 1) * N_TILE],
+                    out=unit[q][:, a, h * N_TILE : (h + 1) * N_TILE],
                     in0=y[i][h][:],
                     scalar1=rnorm[i][:, 0:1],
                     scalar2=None,
                     op0=ALU.mult,
                 )
-            nc.sync.dma_start(out=out_pairs[q][:, a, :], in_=unit[:])
+            if q == n_pairs - 1:
+                nc.sync.dma_start(out=out_blocks[b][:, t, :], in_=unit[q][:, a, :])
+            elif a == PAIR - 1:
+                nc.sync.dma_start(out=out_blocks[b][:, t - a : t + 1, :], in_=unit[q][:])
 
+        for b in range(n_blocks):
+            x_raw[b] = x_in.tile([P, BLOCK, K], BF16, name="x_raw")
         for j in range(W_TILES // HALVES):
             load_w(j)
-        load_pair(0)
+        load_rows(0, 0, PAIR)
         for j in range(W_TILES // HALVES, W_TILES):
             load_w(j)
-        for q in range(1, X_AHEAD):
-            load_pair(q)
+        load_rows(0, PAIR, BLOCK)
+        for b in range(1, n_blocks):
+            load_rows(b, 0, BLOCK)
 
         prepare_weights(0)
         transposes(0)
@@ -199,8 +212,6 @@ def tile_minerva_old_pa_kernel(tc, features, ex_features, g_weight, out_0, out_1
             multiply(i)
             norm(i)
             if a == 0:
-                if q + X_AHEAD < n_pairs:
-                    load_pair(q + X_AHEAD)
                 if q + 2 < n_pairs:
                     transposes(q + 2)
                 if q + 1 < n_pairs:

from contextlib import ExitStack

import concourse.mybir as mybir
from concourse.masks import make_identity

F32 = mybir.dt.float32
BF16 = mybir.dt.bfloat16
U32 = mybir.dt.uint32
U8 = mybir.dt.uint8
FP8X4 = mybir.dt.float8_e4m3fn_x4
ACT = mybir.ActivationFunctionType
ALU = mybir.AluOpType

P = 128
PACK = 4
K = 1024
K_PASS = P * PACK
PASSES = K // K_PASS
F_OUT = 1024
N_TILE = 512
HALVES = F_OUT // N_TILE
W_TILES = F_OUT // P
PAIR = 2
BLOCK = 4
PLANES = K // 2 // P
TILE_WORDS = PASSES * P
EPS = 1e-12

FLOPS = 2 * (1024 + 4096) * K * F_OUT


def tile_minerva_old_pa_kernel(tc, features, ex_features, g_weight, out_0, out_1):
    nc = tc.nc

    x_blocks = []
    out_blocks = []
    for x, out in ((features, out_0), (ex_features, out_1)):
        x_view = x.rearrange("(b p t) k -> b p t k", p=P, t=BLOCK)
        out_view = out.rearrange("(b p t) f -> b p t f", p=P, t=BLOCK)
        for b in range(x.shape[0] // (P * BLOCK)):
            x_blocks.append(x_view[b])
            out_blocks.append(out_view[b])
    n_blocks = len(x_blocks)
    n_tiles = n_blocks * BLOCK
    n_pairs = n_tiles // PAIR
    w_rows = g_weight.rearrange("(j p) k -> j p k", p=P)

    with ExitStack() as ctx:
        ctx.enter_context(tc.manual_schedule())
        const = ctx.enter_context(tc.tile_pool(name="const", bufs=1))
        w_in = ctx.enter_context(tc.tile_pool(name="w_in", bufs=W_TILES))
        x_in = ctx.enter_context(tc.tile_pool(name="x_in", bufs=n_blocks))
        stage = ctx.enter_context(tc.tile_pool(name="stage", bufs=3))
        small = ctx.enter_context(tc.tile_pool(name="small", bufs=4))
        result = ctx.enter_context(tc.tile_pool(name="result", bufs=6))
        psum_t = ctx.enter_context(tc.psum_pool(name="psum_t", bufs=2))
        psum_y = ctx.enter_context(tc.psum_pool(name="psum_y", bufs=6))

        ident = const.tile([P, P], F32, name="ident")
        make_identity(nc, ident[:])
        neg_half = const.tile([P, 1], F32, name="neg_half")
        nc.gpsimd.memset(neg_half[:], -0.5)

        w_grouped = const.tile([P, PASSES * F_OUT * PACK], BF16, name="w_grouped", align_bytes=64)
        w_codes = const.tile([P, PASSES * F_OUT], U32, name="w_codes", align_bytes=64)
        w_scales = const.tile([P, PASSES * F_OUT], U8, name="w_scales", align_bytes=64)

        w_raw = {}
        x_raw = {}
        banks = {}
        grouped = {}
        codes = {}
        scales = {}
        y = {}
        sumsq = {}
        rnorm = {}
        unit = {}

        def load_w(j):
            w_raw[j] = w_in.tile([P, K], BF16, name="w_raw")
            nc.sync.dma_start(out=w_raw[j][:], in_=w_rows[j])

        def load_rows(b, t_lo, t_hi):
            nc.sync.dma_start(out=x_raw[b][:, t_lo:t_hi, :], in_=x_blocks[b][:, t_lo:t_hi, :])

        def transpose_words(rows, bank):
            words = rows.bitcast(F32)
            for c in range(PLANES):
                nc.tensor.transpose(bank[:, c, :], words[:, c * P : (c + 1) * P], ident[:])

        def by_row(bank):
            return bank[:].rearrange("p (g u) r -> p g r u", u=2)

        def prepare_weights(h):
            dest = w_grouped[:].bitcast(F32).rearrange("p (g f u) -> p g f u", g=PASSES, u=2)
            for j in range(h * W_TILES // HALVES, (h + 1) * W_TILES // HALVES):
                bank = psum_y.tile([P, PLANES, P], F32, name="w_bank", tag="acc")
                transpose_words(w_raw[j][:], bank)
                if j % 2 == 0:
                    nc.vector.tensor_copy(out=dest[:, :, j * P : (j + 1) * P, :], in_=by_row(bank))
                else:
                    nc.scalar.copy(out=dest[:, :, j * P : (j + 1) * P, :], in_=by_row(bank))
                for g in range(PASSES):
                    lo = g * F_OUT + j * P
                    nc.vector.quantize_mx(
                        out=w_codes[:, lo : lo + P].bitcast(FP8X4),
                        scales=w_scales[:, lo : lo + P],
                        in_=w_grouped[:, lo * PACK : (lo + P) * PACK],
                    )

        def transposes(q):
            banks[q] = []
            for a in range(PAIR):
                bank = psum_t.tile([P, PLANES, P], F32, name="bank")
                b, t = divmod(q * PAIR + a, BLOCK)
                transpose_words(x_raw[b][:, t, :], bank)
                banks[q].append(bank)

        def regroup(q):
            grouped[q] = stage.tile([P, PAIR * TILE_WORDS * PACK], BF16, name="grouped", align_bytes=64)
            dest = grouped[q][:].bitcast(F32).rearrange("p (a g r u) -> p a g r u", a=PAIR, g=PASSES, u=2)
            for a in range(PAIR):
                if (q * PAIR + a) % 4 == 0:
                    nc.vector.tensor_copy(out=dest[:, a], in_=by_row(banks[q][a]))
                else:
                    nc.scalar.copy(out=dest[:, a], in_=by_row(banks[q][a]))

        def quantise(q):
            codes[q] = stage.tile([P, PAIR * TILE_WORDS], U32, name="codes", align_bytes=64)
            scales[q] = stage.tile([P, PAIR * TILE_WORDS], U8, name="scales", align_bytes=64)
            nc.vector.quantize_mx(
                out=codes[q][:].bitcast(FP8X4), scales=scales[q][:], in_=grouped[q][:]
            )

        def multiply(i):
            q, a = divmod(i, PAIR)
            y[i] = []
            for h in range(HALVES):
                acc = psum_y.tile([P, N_TILE], F32, name="acc")
                for g in range(PASSES):
                    rows = slice(a * TILE_WORDS + g * P, a * TILE_WORDS + (g + 1) * P)
                    cols = slice(g * F_OUT + h * N_TILE, g * F_OUT + (h + 1) * N_TILE)
                    nc.tensor.matmul_mx(
                        out=acc[:],
                        lhsT=codes[q][:, rows].bitcast(FP8X4),
                        lhsT_scale=scales[q][:, rows],
                        rhs=w_codes[:, cols].bitcast(FP8X4),
                        rhs_scale=w_scales[:, cols],
                        start=(g == 0),
                        stop=(g == PASSES - 1),
                    )
                y[i].append(acc)

        def norm(i):
            sumsq[i] = small.tile([P, HALVES], F32, name="sumsq")
            for h in range(HALVES):
                squares = stage.tile([P, N_TILE], F32, name="squares")
                nc.scalar.activation(
                    out=squares[:], in_=y[i][h][:], func=ACT.Square, accum_out=sumsq[i][:, h : h + 1]
                )
            clamped = small.tile([P, 1], F32, name="clamped")
            nc.gpsimd.tensor_scalar(
                out=clamped[:],
                in0=sumsq[i][:, 0:1],
                scalar1=sumsq[i][:, 1:2],
                scalar2=EPS * EPS,
                op0=ALU.add,
                op1=ALU.max,
            )
            rnorm[i] = small.tile([P, 1], F32, name="rnorm")
            nc.gpsimd.tensor_tensor(out=rnorm[i][:], in0=clamped[:], in1=neg_half[:], op=ALU.pow)

        def scale_and_store(i):
            q, a = divmod(i, PAIR)
            b, t = divmod(i, BLOCK)
            if a == 0:
                unit[q] = result.tile([P, PAIR, F_OUT], F32, name="unit")
            for h in range(HALVES):
                nc.vector.tensor_scalar(
                    out=unit[q][:, a, h * N_TILE : (h + 1) * N_TILE],
                    in0=y[i][h][:],
                    scalar1=rnorm[i][:, 0:1],
                    scalar2=None,
                    op0=ALU.mult,
                )
            if q == n_pairs - 1:
                nc.sync.dma_start(out=out_blocks[b][:, t, :], in_=unit[q][:, a, :])
            elif a == PAIR - 1:
                nc.sync.dma_start(out=out_blocks[b][:, t - a : t + 1, :], in_=unit[q][:])

        for b in range(n_blocks):
            x_raw[b] = x_in.tile([P, BLOCK, K], BF16, name="x_raw")
        for j in range(W_TILES // HALVES):
            load_w(j)
        load_rows(0, 0, PAIR)
        for j in range(W_TILES // HALVES, W_TILES):
            load_w(j)
        load_rows(0, PAIR, BLOCK)
        for b in range(1, n_blocks):
            load_rows(b, 0, BLOCK)

        prepare_weights(0)
        transposes(0)
        regroup(0)
        quantise(0)
        prepare_weights(1)
        transposes(1)
        regroup(1)

        for i in range(n_tiles):
            q, a = divmod(i, PAIR)
            multiply(i)
            norm(i)
            if a == 0:
                if q + 2 < n_pairs:
                    transposes(q + 2)
                if q + 1 < n_pairs:
                    quantise(q + 1)
            if i >= 1:
                scale_and_store(i - 1)
            if a == 0 and q + 2 < n_pairs:
                regroup(q + 2)
        scale_and_store(n_tiles - 1)
